import numpy as np
import ml_dtypes

BF16 = ml_dtypes.bfloat16


def bf(x):
    return np.asarray(x, np.float32).astype(BF16)


def f32(x):
    return np.asarray(x, np.float32)


def f64(x):
    return np.asarray(x).astype(np.float64)


def striped(idx):
    return np.tile(idx.reshape(-1, 16).T, (8, 1))


C, S, N, D = 512, 512, 128, 128
ALPHA = 0.1
KEEP = 0.95


def setup_inputs():
    base = f32(0.3 * np.random.standard_normal((C, S)))
    h = bf(np.random.standard_normal((S, C)))
    a = np.random.uniform(size=(N, S))
    a = np.where(a > KEEP, a, 0.0)
    a = a / a.sum(axis=1, keepdims=True)
    adj_t = bf(a.T)
    x0 = bf(np.random.standard_normal((D, N)))
    w0 = bf(np.random.standard_normal((D, C)) / np.sqrt(D))
    return {"base": base, "h": h, "adj_t": adj_t, "x0": x0, "w0": w0, "offs": striped(np.random.permutation(S)[:N])}


def reference(base, h, adj_t, x0, w0, offs):
    idx = offs[:16].T.reshape(-1)
    prop = f64(h).T @ f64(adj_t)
    h0 = f64(w0).T @ f64(x0)
    out = f64(base).copy()
    out[:, idx] = (1.0 - ALPHA) * prop + ALPHA * h0
    return out

@@ -1,0 +1,55 @@
+import concourse.mybir as mybir
+
+P = 128
+C, S, N, D = 512, 512, 128, 128
+C_BLOCKS = C // P
+M_BLOCKS = S // P
+ALPHA = 0.1
+
+FLOPS = 2 * C * S * N + 2 * C * D * N
+
+BF16, F32, U16 = mybir.dt.bfloat16, mybir.dt.float32, mybir.dt.uint16
+
+
+def tile_graphconv_kernel(tc, base, h, adj_t, x0, w0, offs, out):
+    nc = tc.nc
+    with (
+        tc.tile_pool(name="held", bufs=1) as held,
+        tc.tile_pool(name="terms", bufs=2) as terms,
+        tc.psum_pool(name="psum", bufs=1) as psum,
+    ):
+        offsets = held.tile([P, N // 16], U16, name="offsets")
+        nc.sync.dma_start(offsets[:], offs)
+
+        adj_sb = held.tile([P, M_BLOCKS, N], BF16, name="adj_sb")
+        nc.sync.dma_start(adj_sb[:], adj_t.rearrange("(p k) j -> p k j", k=M_BLOCKS))
+        h_sb = held.tile([P, M_BLOCKS, C], BF16, name="h_sb")
+        nc.sync.dma_start(h_sb[:], h.rearrange("(p k) c -> p k c", k=M_BLOCKS))
+
+        x0_sb = held.tile([P, N], BF16, name="x0_sb")
+        nc.scalar.dma_start(x0_sb[:], x0)
+        w0_sb = held.tile([P, C], BF16, name="w0_sb")
+        nc.scalar.dma_start(w0_sb[:], w0)
+
+        windows = [held.tile([P, S], F32, name=f"window{cb}") for cb in range(C_BLOCKS)]
+        for cb in range(C_BLOCKS):
+            nc.scalar.dma_start(windows[cb][:], base[cb * P : (cb + 1) * P, :])
+
+        for cb in range(C_BLOCKS):
+            channels = slice(cb * P, (cb + 1) * P)
+
+            teleport_ps = psum.tile([P, N], F32, name=f"teleport_ps{cb}")
+            nc.tensor.matmul(teleport_ps[:], w0_sb[:, channels], x0_sb[:], start=True, stop=True)
+            teleport = terms.tile([P, N], F32, name="teleport")
+            nc.scalar.mul(teleport[:], teleport_ps[:], ALPHA)
+
+            prop_ps = psum.tile([P, N], F32, name=f"prop_ps{cb}")
+            for k in range(M_BLOCKS):
+                nc.tensor.matmul(
+                    prop_ps[:], h_sb[:, k, channels], adj_sb[:, k, :], start=(k == 0), stop=(k == M_BLOCKS - 1)
+                )
+            prop = terms.tile([P, N], F32, name="prop")
+            nc.scalar.mul(prop[:], prop_ps[:], 1.0 - ALPHA)
+
+            nc.vector.tensor_tensor(windows[cb][:].indirect(offsets[:]), prop[:], teleport[:], mybir.AluOpType.add)
+            nc.sync.dma_start(out[channels, :], windows[cb][:])

@@ -19,30 +19,34 @@ def tile_graphconv_kernel(tc, base, h, adj_t, x0, w0, offs, out):
         tc.psum_pool(name="psum", bufs=1) as psum,
     ):
         offsets = held.tile([P, N // 16], U16, name="offsets")
-        nc.sync.dma_start(offsets[:], offs)
-
-        adj_sb = held.tile([P, M_BLOCKS, N], BF16, name="adj_sb")
-        nc.sync.dma_start(adj_sb[:], adj_t.rearrange("(p k) j -> p k j", k=M_BLOCKS))
         h_sb = held.tile([P, M_BLOCKS, C], BF16, name="h_sb")
-        nc.sync.dma_start(h_sb[:], h.rearrange("(p k) c -> p k c", k=M_BLOCKS))
-
+        h_view = h.rearrange("(p k) c -> p k c", k=M_BLOCKS)
+        adj_sb = held.tile([P, M_BLOCKS, N], BF16, name="adj_sb")
+        adj_view = adj_t.rearrange("(p k) j -> p k j", k=M_BLOCKS)
         x0_sb = held.tile([P, N], BF16, name="x0_sb")
-        nc.scalar.dma_start(x0_sb[:], x0)
         w0_sb = held.tile([P, C], BF16, name="w0_sb")
-        nc.scalar.dma_start(w0_sb[:], w0)
-
         windows = [held.tile([P, S], F32, name=f"window{cb}") for cb in range(C_BLOCKS)]
+
+        HALF = C // 2
+        nc.sync.dma_start(offsets[:], offs)
+        nc.scalar.dma_start(x0_sb[:], x0)
+        nc.sync.dma_start(adj_sb[:], adj_view)
+        nc.scalar.dma_start(w0_sb[:], w0)
+        nc.sync.dma_start(h_sb[:, :, :HALF], h_view[:, :, :HALF])
+        nc.scalar.dma_start(windows[0][:], base[0 * P : 1 * P, :])
+        nc.sync.dma_start(h_sb[:, :, HALF:], h_view[:, :, HALF:])
+        nc.scalar.dma_start(windows[1][:], base[1 * P : 2 * P, :])
+        nc.sync.dma_start(windows[2][:], base[2 * P : 3 * P, :])
+        nc.sync.dma_start(windows[3][:], base[3 * P : 4 * P, :])
+
+        teleport_ps = psum.tile([P, C_BLOCKS, N], F32, name="teleport_ps")
         for cb in range(C_BLOCKS):
-            nc.scalar.dma_start(windows[cb][:], base[cb * P : (cb + 1) * P, :])
+            nc.tensor.matmul(teleport_ps[:, cb, :], w0_sb[:, cb * P : (cb + 1) * P], x0_sb[:], start=True, stop=True)
+        teleport = held.tile([P, C_BLOCKS, N], F32, name="teleport")
+        nc.vector.tensor_scalar_mul(teleport[:], teleport_ps[:], ALPHA)
 
         for cb in range(C_BLOCKS):
             channels = slice(cb * P, (cb + 1) * P)
-
-            teleport_ps = psum.tile([P, N], F32, name=f"teleport_ps{cb}")
-            nc.tensor.matmul(teleport_ps[:], w0_sb[:, channels], x0_sb[:], start=True, stop=True)
-            teleport = terms.tile([P, N], F32, name="teleport")
-            nc.scalar.mul(teleport[:], teleport_ps[:], ALPHA)
-
             prop_ps = psum.tile([P, N], F32, name=f"prop_ps{cb}")
             for k in range(M_BLOCKS):
                 nc.tensor.matmul(
@@ -51,5 +55,7 @@ def tile_graphconv_kernel(tc, base, h, adj_t, x0, w0, offs, out):
             prop = terms.tile([P, N], F32, name="prop")
             nc.scalar.mul(prop[:], prop_ps[:], 1.0 - ALPHA)
 
-            nc.vector.tensor_tensor(windows[cb][:].indirect(offsets[:]), prop[:], teleport[:], mybir.AluOpType.add)
+            nc.vector.tensor_tensor(
+                windows[cb][:].indirect(offsets[:]), prop[:], teleport[:, cb, :], mybir.AluOpType.add
+            )
             nc.sync.dma_start(out[channels, :], windows[cb][:])

@@ -28,25 +28,20 @@ def tile_graphconv_kernel(tc, base, h, adj_t, x0, w0, offs, out):
         windows = [held.tile([P, S], F32, name=f"window{cb}") for cb in range(C_BLOCKS)]
 
         HALF = C // 2
-        nc.sync.dma_start(offsets[:], offs)
-        nc.scalar.dma_start(x0_sb[:], x0)
         nc.sync.dma_start(adj_sb[:], adj_view)
-        nc.scalar.dma_start(w0_sb[:], w0)
+        nc.scalar.dma_start(x0_sb[:], x0)
         nc.sync.dma_start(h_sb[:, :, :HALF], h_view[:, :, :HALF])
+        nc.scalar.dma_start(w0_sb[:], w0)
+        nc.sync.dma_start(offsets[:], offs)
         nc.scalar.dma_start(windows[0][:], base[0 * P : 1 * P, :])
         nc.sync.dma_start(h_sb[:, :, HALF:], h_view[:, :, HALF:])
         nc.scalar.dma_start(windows[1][:], base[1 * P : 2 * P, :])
         nc.sync.dma_start(windows[2][:], base[2 * P : 3 * P, :])
         nc.sync.dma_start(windows[3][:], base[3 * P : 4 * P, :])
 
-        teleport_ps = psum.tile([P, C_BLOCKS, N], F32, name="teleport_ps")
-        for cb in range(C_BLOCKS):
-            nc.tensor.matmul(teleport_ps[:, cb, :], w0_sb[:, cb * P : (cb + 1) * P], x0_sb[:], start=True, stop=True)
-        teleport = held.tile([P, C_BLOCKS, N], F32, name="teleport")
-        nc.vector.tensor_scalar_mul(teleport[:], teleport_ps[:], ALPHA)
-
         for cb in range(C_BLOCKS):
             channels = slice(cb * P, (cb + 1) * P)
+
             prop_ps = psum.tile([P, N], F32, name=f"prop_ps{cb}")
             for k in range(M_BLOCKS):
                 nc.tensor.matmul(
@@ -55,7 +50,10 @@ def tile_graphconv_kernel(tc, base, h, adj_t, x0, w0, offs, out):
             prop = terms.tile([P, N], F32, name="prop")
             nc.scalar.mul(prop[:], prop_ps[:], 1.0 - ALPHA)
 
-            nc.vector.tensor_tensor(
-                windows[cb][:].indirect(offsets[:]), prop[:], teleport[:, cb, :], mybir.AluOpType.add
-            )
+            teleport_ps = psum.tile([P, N], F32, name=f"teleport_ps{cb}")
+            nc.tensor.matmul(teleport_ps[:], w0_sb[:, channels], x0_sb[:], start=True, stop=True)
+            teleport = terms.tile([P, N], F32, name="teleport")
+            nc.scalar.mul(teleport[:], teleport_ps[:], ALPHA)
+
+            nc.vector.tensor_tensor(windows[cb][:].indirect(offsets[:]), prop[:], teleport[:], mybir.AluOpType.add)
             nc.sync.dma_start(out[channels, :], windows[cb][:])

@@ -37,7 +37,7 @@ def tile_graphconv_kernel(tc, base, h, adj_t, x0, w0, offs, out):
         nc.sync.dma_start(h_sb[:, :, HALF:], h_view[:, :, HALF:])
         nc.scalar.dma_start(windows[1][:], base[1 * P : 2 * P, :])
         nc.sync.dma_start(windows[2][:], base[2 * P : 3 * P, :])
-        nc.sync.dma_start(windows[3][:], base[3 * P : 4 * P, :])
+        nc.gpsimd.dma_start(windows[3][:], base[3 * P : 4 * P, :])
 
         for cb in range(C_BLOCKS):
             channels = slice(cb * P, (cb + 1) * P)

@@ -9,6 +9,7 @@ ALPHA = 0.1
 FLOPS = 2 * C * S * N + 2 * C * D * N
 
 BF16, F32, U16 = mybir.dt.bfloat16, mybir.dt.float32, mybir.dt.uint16
+WARM_MATMULS = 4
 
 
 def tile_graphconv_kernel(tc, base, h, adj_t, x0, w0, offs, out):
@@ -16,7 +17,8 @@ def tile_graphconv_kernel(tc, base, h, adj_t, x0, w0, offs, out):
     with (
         tc.tile_pool(name="held", bufs=1) as held,
         tc.tile_pool(name="terms", bufs=2) as terms,
-        tc.psum_pool(name="psum", bufs=1) as psum,
+        tc.psum_pool(name="psum", bufs=2) as psum,
+        tc.psum_pool(name="idle", bufs=1) as idle,
     ):
         offsets = held.tile([P, N // 16], U16, name="offsets")
         h_sb = held.tile([P, M_BLOCKS, C], BF16, name="h_sb")
@@ -37,12 +39,18 @@ def tile_graphconv_kernel(tc, base, h, adj_t, x0, w0, offs, out):
         nc.sync.dma_start(h_sb[:, :, HALF:], h_view[:, :, HALF:])
         nc.scalar.dma_start(windows[1][:], base[1 * P : 2 * P, :])
         nc.sync.dma_start(windows[2][:], base[2 * P : 3 * P, :])
-        nc.gpsimd.dma_start(windows[3][:], base[3 * P : 4 * P, :])
+        nc.sync.dma_start(windows[3][:], base[3 * P : 4 * P, :])
+
+        zeros = held.tile([P, C], BF16, name="zeros")
+        nc.vector.memset(zeros[:], 0.0)
+        unread_ps = idle.tile([P, C], F32, name="unread_ps")
+        for i in range(WARM_MATMULS):
+            nc.tensor.matmul(unread_ps[:], zeros[:, :P], zeros[:], start=True, stop=True)
 
         for cb in range(C_BLOCKS):
             channels = slice(cb * P, (cb + 1) * P)
 
-            prop_ps = psum.tile([P, N], F32, name=f"prop_ps{cb}")
+            prop_ps = psum.tile([P, N], F32, name="prop_ps")
             for k in range(M_BLOCKS):
                 nc.tensor.matmul(
                     prop_ps[:], h_sb[:, k, channels], adj_sb[:, k, :], start=(k == 0), stop=(k == M_BLOCKS - 1)
@@ -50,7 +58,7 @@ def tile_graphconv_kernel(tc, base, h, adj_t, x0, w0, offs, out):
             prop = terms.tile([P, N], F32, name="prop")
             nc.scalar.mul(prop[:], prop_ps[:], 1.0 - ALPHA)
 
-            teleport_ps = psum.tile([P, N], F32, name=f"teleport_ps{cb}")
+            teleport_ps = psum.tile([P, N], F32, name="teleport_ps")
             nc.tensor.matmul(teleport_ps[:], w0_sb[:, channels], x0_sb[:], start=True, stop=True)
             teleport = terms.tile([P, N], F32, name="teleport")
             nc.scalar.mul(teleport[:], teleport_ps[:], ALPHA)

@@ -9,7 +9,6 @@ ALPHA = 0.1
 FLOPS = 2 * C * S * N + 2 * C * D * N
 
 BF16, F32, U16 = mybir.dt.bfloat16, mybir.dt.float32, mybir.dt.uint16
-WARM_MATMULS = 4
 
 
 def tile_graphconv_kernel(tc, base, h, adj_t, x0, w0, offs, out):
@@ -17,8 +16,7 @@ def tile_graphconv_kernel(tc, base, h, adj_t, x0, w0, offs, out):
     with (
         tc.tile_pool(name="held", bufs=1) as held,
         tc.tile_pool(name="terms", bufs=2) as terms,
-        tc.psum_pool(name="psum", bufs=2) as psum,
-        tc.psum_pool(name="idle", bufs=1) as idle,
+        tc.psum_pool(name="psum", bufs=1) as psum,
     ):
         offsets = held.tile([P, N // 16], U16, name="offsets")
         h_sb = held.tile([P, M_BLOCKS, C], BF16, name="h_sb")
@@ -29,28 +27,20 @@ def tile_graphconv_kernel(tc, base, h, adj_t, x0, w0, offs, out):
         w0_sb = held.tile([P, C], BF16, name="w0_sb")
         windows = [held.tile([P, S], F32, name=f"window{cb}") for cb in range(C_BLOCKS)]
 
-        HALF = C // 2
         nc.sync.dma_start(adj_sb[:], adj_view)
         nc.scalar.dma_start(x0_sb[:], x0)
-        nc.sync.dma_start(h_sb[:, :, :HALF], h_view[:, :, :HALF])
+        nc.sync.dma_start(h_sb[:], h_view)
         nc.scalar.dma_start(w0_sb[:], w0)
         nc.sync.dma_start(offsets[:], offs)
         nc.scalar.dma_start(windows[0][:], base[0 * P : 1 * P, :])
-        nc.sync.dma_start(h_sb[:, :, HALF:], h_view[:, :, HALF:])
         nc.scalar.dma_start(windows[1][:], base[1 * P : 2 * P, :])
         nc.sync.dma_start(windows[2][:], base[2 * P : 3 * P, :])
         nc.sync.dma_start(windows[3][:], base[3 * P : 4 * P, :])
 
-        zeros = held.tile([P, C], BF16, name="zeros")
-        nc.vector.memset(zeros[:], 0.0)
-        unread_ps = idle.tile([P, C], F32, name="unread_ps")
-        for i in range(WARM_MATMULS):
-            nc.tensor.matmul(unread_ps[:], zeros[:, :P], zeros[:], start=True, stop=True)
-
         for cb in range(C_BLOCKS):
             channels = slice(cb * P, (cb + 1) * P)
 
-            prop_ps = psum.tile([P, N], F32, name="prop_ps")
+            prop_ps = psum.tile([P, N], F32, name=f"prop_ps{cb}")
             for k in range(M_BLOCKS):
                 nc.tensor.matmul(
                     prop_ps[:], h_sb[:, k, channels], adj_sb[:, k, :], start=(k == 0), stop=(k == M_BLOCKS - 1)
@@ -58,7 +48,7 @@ def tile_graphconv_kernel(tc, base, h, adj_t, x0, w0, offs, out):
             prop = terms.tile([P, N], F32, name="prop")
             nc.scalar.mul(prop[:], prop_ps[:], 1.0 - ALPHA)
 
-            teleport_ps = psum.tile([P, N], F32, name="teleport_ps")
+            teleport_ps = psum.tile([P, N], F32, name=f"teleport_ps{cb}")
             nc.tensor.matmul(teleport_ps[:], w0_sb[:, channels], x0_sb[:], start=True, stop=True)
             teleport = terms.tile([P, N], F32, name="teleport")
             nc.scalar.mul(teleport[:], teleport_ps[:], ALPHA)

@@ -15,7 +15,6 @@ def tile_graphconv_kernel(tc, base, h, adj_t, x0, w0, offs, out):
     nc = tc.nc
     with (
         tc.tile_pool(name="held", bufs=1) as held,
-        tc.tile_pool(name="terms", bufs=2) as terms,
         tc.psum_pool(name="psum", bufs=1) as psum,
     ):
         offsets = held.tile([P, N // 16], U16, name="offsets")
@@ -27,13 +26,17 @@ def tile_graphconv_kernel(tc, base, h, adj_t, x0, w0, offs, out):
         w0_sb = held.tile([P, C], BF16, name="w0_sb")
         windows = [held.tile([P, S], F32, name=f"window{cb}") for cb in range(C_BLOCKS)]
 
+        C_HALF = C // 2
+        K_HALF = M_BLOCKS // 2
         nc.sync.dma_start(adj_sb[:], adj_view)
-        nc.scalar.dma_start(x0_sb[:], x0)
-        nc.sync.dma_start(h_sb[:], h_view)
+        nc.scalar.dma_start(h_sb[:, :K_HALF, :C_HALF], h_view[:, :K_HALF, :C_HALF])
+        nc.sync.dma_start(h_sb[:, K_HALF:, :C_HALF], h_view[:, K_HALF:, :C_HALF])
         nc.scalar.dma_start(w0_sb[:], w0)
-        nc.sync.dma_start(offsets[:], offs)
+        nc.sync.dma_start(x0_sb[:], x0)
         nc.scalar.dma_start(windows[0][:], base[0 * P : 1 * P, :])
-        nc.scalar.dma_start(windows[1][:], base[1 * P : 2 * P, :])
+        nc.sync.dma_start(offsets[:], offs)
+        nc.sync.dma_start(h_sb[:, :, C_HALF:], h_view[:, :, C_HALF:])
+        nc.sync.dma_start(windows[1][:], base[1 * P : 2 * P, :])
         nc.sync.dma_start(windows[2][:], base[2 * P : 3 * P, :])
         nc.sync.dma_start(windows[3][:], base[3 * P : 4 * P, :])
 
@@ -45,12 +48,12 @@ def tile_graphconv_kernel(tc, base, h, adj_t, x0, w0, offs, out):
                 nc.tensor.matmul(
                     prop_ps[:], h_sb[:, k, channels], adj_sb[:, k, :], start=(k == 0), stop=(k == M_BLOCKS - 1)
                 )
-            prop = terms.tile([P, N], F32, name="prop")
+            prop = held.tile([P, N], F32, name=f"prop{cb}")
             nc.scalar.mul(prop[:], prop_ps[:], 1.0 - ALPHA)
 
             teleport_ps = psum.tile([P, N], F32, name=f"teleport_ps{cb}")
             nc.tensor.matmul(teleport_ps[:], w0_sb[:, channels], x0_sb[:], start=True, stop=True)
-            teleport = terms.tile([P, N], F32, name="teleport")
+            teleport = held.tile([P, N], F32, name=f"teleport{cb}")
             nc.scalar.mul(teleport[:], teleport_ps[:], ALPHA)
 
             nc.vector.tensor_tensor(windows[cb][:].indirect(offsets[:]), prop[:], teleport[:], mybir.AluOpType.add)

@@ -5,6 +5,7 @@ C, S, N, D = 512, 512, 128, 128
 C_BLOCKS = C // P
 M_BLOCKS = S // P
 ALPHA = 0.1
+DMA_ALIGN = 256
 
 FLOPS = 2 * C * S * N + 2 * C * D * N
 
@@ -18,13 +19,13 @@ def tile_graphconv_kernel(tc, base, h, adj_t, x0, w0, offs, out):
         tc.psum_pool(name="psum", bufs=1) as psum,
     ):
         offsets = held.tile([P, N // 16], U16, name="offsets")
-        h_sb = held.tile([P, M_BLOCKS, C], BF16, name="h_sb")
+        h_sb = held.tile([P, M_BLOCKS, C], BF16, name="h_sb", align_bytes=DMA_ALIGN)
         h_view = h.rearrange("(p k) c -> p k c", k=M_BLOCKS)
-        adj_sb = held.tile([P, M_BLOCKS, N], BF16, name="adj_sb")
+        adj_sb = held.tile([P, M_BLOCKS, N], BF16, name="adj_sb", align_bytes=DMA_ALIGN)
         adj_view = adj_t.rearrange("(p k) j -> p k j", k=M_BLOCKS)
-        x0_sb = held.tile([P, N], BF16, name="x0_sb")
-        w0_sb = held.tile([P, C], BF16, name="w0_sb")
-        windows = [held.tile([P, S], F32, name=f"window{cb}") for cb in range(C_BLOCKS)]
+        x0_sb = held.tile([P, N], BF16, name="x0_sb", align_bytes=DMA_ALIGN)
+        w0_sb = held.tile([P, C], BF16, name="w0_sb", align_bytes=DMA_ALIGN)
+        windows = [held.tile([P, S], F32, name=f"window{cb}", align_bytes=DMA_ALIGN) for cb in range(C_BLOCKS)]
 
         C_HALF = C // 2
         K_HALF = M_BLOCKS // 2

@@ -5,7 +5,7 @@ C, S, N, D = 512, 512, 128, 128
 C_BLOCKS = C // P
 M_BLOCKS = S // P
 ALPHA = 0.1
-DMA_ALIGN = 256
+DMA_ALIGN = 4096
 
 FLOPS = 2 * C * S * N + 2 * C * D * N
 

@@ -41,21 +41,35 @@ def tile_graphconv_kernel(tc, base, h, adj_t, x0, w0, offs, out):
         nc.sync.dma_start(windows[2][:], base[2 * P : 3 * P, :])
         nc.sync.dma_start(windows[3][:], base[3 * P : 4 * P, :])
 
-        for cb in range(C_BLOCKS):
-            channels = slice(cb * P, (cb + 1) * P)
-
-            prop_ps = psum.tile([P, N], F32, name=f"prop_ps{cb}")
+        def propagate(product, cb):
             for k in range(M_BLOCKS):
                 nc.tensor.matmul(
-                    prop_ps[:], h_sb[:, k, channels], adj_sb[:, k, :], start=(k == 0), stop=(k == M_BLOCKS - 1)
+                    product,
+                    h_sb[:, k, cb * P : (cb + 1) * P],
+                    adj_sb[:, k, :],
+                    start=(k == 0),
+                    stop=(k == M_BLOCKS - 1),
                 )
+
+        def teleport(product, cb):
+            nc.tensor.matmul(product, w0_sb[:, cb * P : (cb + 1) * P], x0_sb[:], start=True, stop=True)
+
+        def place(cb, prop_product, teleport_product):
             prop = held.tile([P, N], F32, name=f"prop{cb}")
-            nc.scalar.mul(prop[:], prop_ps[:], 1.0 - ALPHA)
+            nc.scalar.mul(prop[:], prop_product, 1.0 - ALPHA)
+            teleported = held.tile([P, N], F32, name=f"teleported{cb}")
+            nc.scalar.mul(teleported[:], teleport_product, ALPHA)
+            nc.vector.tensor_tensor(windows[cb][:].indirect(offsets[:]), prop[:], teleported[:], mybir.AluOpType.add)
+            nc.sync.dma_start(out[cb * P : (cb + 1) * P, :], windows[cb][:])
 
-            teleport_ps = psum.tile([P, N], F32, name=f"teleport_ps{cb}")
-            nc.tensor.matmul(teleport_ps[:], w0_sb[:, channels], x0_sb[:], start=True, stop=True)
-            teleport = held.tile([P, N], F32, name=f"teleport{cb}")
-            nc.scalar.mul(teleport[:], teleport_ps[:], ALPHA)
+        prop_bank = psum.tile([P, N], F32, name="prop_bank")
+        teleport_bank = psum.tile([P, N], F32, name="teleport_bank")
+        propagate(prop_bank[:], 0)
+        teleport(teleport_bank[:], 0)
+        place(0, prop_bank[:], teleport_bank[:])
 
-            nc.vector.tensor_tensor(windows[cb][:].indirect(offsets[:]), prop[:], teleport[:], mybir.AluOpType.add)
-            nc.sync.dma_start(out[channels, :], windows[cb][:])
+        for cb in range(1, C_BLOCKS):
+            bank = psum.tile([P, 2, N], F32, name=f"bank{cb}")
+            teleport(bank[:, 0, :], cb)
+            propagate(bank[:, 1, :], cb)
+            place(cb, bank[:, 1, :], bank[:, 0, :])

import concourse.mybir as mybir

P = 128
C, S, N, D = 512, 512, 128, 128
C_BLOCKS = C // P
M_BLOCKS = S // P
ALPHA = 0.1
DMA_ALIGN = 4096

FLOPS = 2 * C * S * N + 2 * C * D * N

BF16, F32, U16 = mybir.dt.bfloat16, mybir.dt.float32, mybir.dt.uint16


def tile_graphconv_kernel(tc, base, h, adj_t, x0, w0, offs, out):
    nc = tc.nc
    with (
        tc.tile_pool(name="held", bufs=1) as held,
        tc.psum_pool(name="psum", bufs=1) as psum,
    ):
        offsets = held.tile([P, N // 16], U16, name="offsets")
        h_sb = held.tile([P, M_BLOCKS, C], BF16, name="h_sb", align_bytes=DMA_ALIGN)
        h_view = h.rearrange("(p k) c -> p k c", k=M_BLOCKS)
        adj_sb = held.tile([P, M_BLOCKS, N], BF16, name="adj_sb", align_bytes=DMA_ALIGN)
        adj_view = adj_t.rearrange("(p k) j -> p k j", k=M_BLOCKS)
        x0_sb = held.tile([P, N], BF16, name="x0_sb", align_bytes=DMA_ALIGN)
        w0_sb = held.tile([P, C], BF16, name="w0_sb", align_bytes=DMA_ALIGN)
        windows = [held.tile([P, S], F32, name=f"window{cb}", align_bytes=DMA_ALIGN) for cb in range(C_BLOCKS)]

        C_HALF = C // 2
        K_HALF = M_BLOCKS // 2
        nc.sync.dma_start(adj_sb[:], adj_view)
        nc.scalar.dma_start(h_sb[:, :K_HALF, :C_HALF], h_view[:, :K_HALF, :C_HALF])
        nc.sync.dma_start(h_sb[:, K_HALF:, :C_HALF], h_view[:, K_HALF:, :C_HALF])
        nc.scalar.dma_start(w0_sb[:], w0)
        nc.sync.dma_start(x0_sb[:], x0)
        nc.scalar.dma_start(windows[0][:], base[0 * P : 1 * P, :])
        nc.sync.dma_start(offsets[:], offs)
        nc.sync.dma_start(h_sb[:, :, C_HALF:], h_view[:, :, C_HALF:])
        nc.sync.dma_start(windows[1][:], base[1 * P : 2 * P, :])
        nc.sync.dma_start(windows[2][:], base[2 * P : 3 * P, :])
        nc.sync.dma_start(windows[3][:], base[3 * P : 4 * P, :])

        def propagate(product, cb):
            for k in range(M_BLOCKS):
                nc.tensor.matmul(
                    product,
                    h_sb[:, k, cb * P : (cb + 1) * P],
                    adj_sb[:, k, :],
                    start=(k == 0),
                    stop=(k == M_BLOCKS - 1),
                )

        def teleport(product, cb):
            nc.tensor.matmul(product, w0_sb[:, cb * P : (cb + 1) * P], x0_sb[:], start=True, stop=True)

        def place(cb, prop_product, teleport_product):
            prop = held.tile([P, N], F32, name=f"prop{cb}")
            nc.scalar.mul(prop[:], prop_product, 1.0 - ALPHA)
            teleported = held.tile([P, N], F32, name=f"teleported{cb}")
            nc.scalar.mul(teleported[:], teleport_product, ALPHA)
            nc.vector.tensor_tensor(windows[cb][:].indirect(offsets[:]), prop[:], teleported[:], mybir.AluOpType.add)
            nc.sync.dma_start(out[cb * P : (cb + 1) * P, :], windows[cb][:])

        prop_bank = psum.tile([P, N], F32, name="prop_bank")
        teleport_bank = psum.tile([P, N], F32, name="teleport_bank")
        propagate(prop_bank[:], 0)
        teleport(teleport_bank[:], 0)
        place(0, prop_bank[:], teleport_bank[:])

        for cb in range(1, C_BLOCKS):
            bank = psum.tile([P, 2, N], F32, name=f"bank{cb}")
            teleport(bank[:, 0, :], cb)
            propagate(bank[:, 1, :], cb)
            place(cb, bank[:, 1, :], bank[:, 0, :])
